import numpy as np
import ml_dtypes


def mxq(x, axis, fmt="e4m3"):
    dtype, down = {"e4m3": (ml_dtypes.float8_e4m3fn, 7), "e5m2": (ml_dtypes.float8_e5m2, 14)}[fmt]
    v = np.moveaxis(np.asarray(x, np.float32).astype(ml_dtypes.bfloat16).astype(np.float64), axis, -1)
    blocks = v.reshape(v.shape[:-1] + (-1, 32))
    amax = np.abs(blocks).max(-1, keepdims=True)
    byte = np.maximum(np.where(amax > 0, np.frexp(amax)[1] - 1 + 127, 0) - down, 1)
    scale = np.exp2(byte - 127.0)
    codes = (blocks / scale).astype(np.float32).astype(dtype).astype(np.float64)
    return np.moveaxis((codes * scale).reshape(v.shape), -1, axis)


WIDE = False


def mx_kscale(k):
    if not WIDE:
        return np.ones(k)
    levels = np.array([10, -10, 5, -5, 0])
    if k % 512:
        return np.exp2(np.random.permutation(np.resize(levels, k // 32))).repeat(32)
    a = np.empty((k // 512, 16))
    for p in range(k // 512):
        a[p, :8] = np.random.permutation(np.resize(levels, 8))
        for g in range(8):
            far = levels[np.abs(levels - a[p, g]) >= 10]
            a[p, g + 8] = far[np.random.randint(len(far))]
    return np.exp2(a.ravel()).repeat(32)


BF16 = ml_dtypes.bfloat16


def bf(x):
    return np.asarray(x, np.float32).astype(BF16)


def f64(x):
    return np.asarray(x).astype(np.float64)


N, K, H, A = 128, 2, 256, 5
D = K * H
T = A * H


def sigmoid(v):
    return 1.0 / (1.0 + np.exp(-v))


def setup_inputs():
    s = mx_kscale(D)
    h_mail = np.random.standard_normal((N, K, H)) * s.reshape(K, H)
    c_mail = np.random.standard_normal((N, K, H))
    U_f_w = np.random.standard_normal((T, T)) / np.sqrt(D)
    U_f_w[:D] = U_f_w[:D] / s[:, None]
    U_f_b = np.random.standard_normal(T) * 0.5
    U_iou_w = np.random.standard_normal((3 * H, T)) / np.sqrt(D)
    U_iou_w[:, :D] = U_iou_w[:, :D] / s
    b_iou = np.random.standard_normal((1, 3 * H)) * 0.3
    return {"h_mail": bf(h_mail), "c_mail": bf(c_mail), "U_f_w": bf(U_f_w), "U_f_b": bf(U_f_b), "U_iou_w": bf(U_iou_w), "b_iou": bf(b_iou)}


def reference(h_mail, c_mail, U_f_w, U_f_b, U_iou_w, b_iou):
    n, k, h = h_mail.shape
    d = k * h
    hq = mxq(f64(h_mail).reshape(n, d), 1, "e4m3")
    f = sigmoid((hq @ mxq(f64(U_f_w)[:d, :d], 0, "e4m3")) + f64(U_f_b)[:d])
    c_red = np.sum(f.reshape(n, k, h) * f64(c_mail), axis=1)
    iou = (hq @ mxq(f64(U_iou_w)[:, :d], 1, "e4m3").T) + f64(b_iou)
    i, o, u = np.split(iou, 3, axis=1)
    c = sigmoid(i) * np.tanh(u) + c_red
    h_out = sigmoid(o) * np.tanh(c)
    return h_out, c

@@ -1,0 +1,196 @@
+from contextlib import ExitStack
+
+import concourse.mybir as mybir
+from concourse.masks import make_identity
+
+F32 = mybir.dt.float32
+BF16 = mybir.dt.bfloat16
+U32 = mybir.dt.uint32
+U8 = mybir.dt.uint8
+FP8X4 = mybir.dt.float8_e4m3fn_x4
+ACT = mybir.ActivationFunctionType
+
+P = 128
+PACK = 4
+K = P * PACK
+H = 256
+HALVES = H // P
+
+F0 = 0
+I0 = 4
+O0 = 6
+U0 = 8
+F_TILES = 4
+GATE_TILES = 10
+IU_TILES = (I0, U0, I0 + 1, U0 + 1)
+O_TILES = (O0, O0 + 1)
+
+FLOPS = 2 * P * K * GATE_TILES * P
+BYTES = 2 * (2 * P * K + K * K + K + 3 * H * K + 3 * H) + 4 * 2 * P * H
+
+
+def transpose_words(nc, psum, rows, ident_f32):
+    words = rows.bitcast(F32)
+    wordsT = psum.tile([P, 2, P], F32, tag="wordsT", name="wordsT")
+    for u in range(2):
+        nc.tensor.transpose(wordsT[:, u, :], words[:, u : 2 * P : 2], ident_f32[:])
+    return wordsT
+
+
+def tile_treelstmcell_s_kernel(tc, h_mail, c_mail, U_f_w, U_f_b, U_iou_w, b_iou, out_0, out_1):
+    nc = tc.nc
+    with ExitStack() as ctx:
+        sb = ctx.enter_context(tc.tile_pool(name="sb", bufs=1))
+        ps_in = ctx.enter_context(tc.psum_pool(name="ps_in", bufs=2))
+        ps_keep = ctx.enter_context(tc.psum_pool(name="ps_keep", bufs=1))
+        ps_bank = ctx.enter_context(tc.psum_pool(name="ps_bank", bufs=5))
+        ctx.enter_context(tc.manual_schedule())
+
+        bias_rows = sb.tile([P, P], BF16)
+        nc.vector.memset(bias_rows[:], 0.0)
+        nc.scalar.dma_start(out=bias_rows[F0:I0, :], in_=U_f_b[0:K].rearrange("(a p) -> a p", p=P))
+        nc.scalar.dma_start(out=bias_rows[I0:GATE_TILES, :], in_=b_iou.rearrange("o (a p) -> (o a) p", p=P))
+
+        h_rows = sb.tile([P, K], BF16)
+        nc.sync.dma_start(out=h_rows[:], in_=h_mail.rearrange("n k h -> n (k h)"))
+        c_rows = sb.tile([P, K], BF16)
+        nc.sync.dma_start(out=c_rows[:], in_=c_mail.rearrange("n k h -> n (k h)"))
+        uf_rows = sb.tile([P, PACK, K], BF16)
+        for u in range(2):
+            nc.sync.dma_start(
+                out=uf_rows[:, 2 * u : 2 * u + 2, :],
+                in_=U_f_w[0:K, 0:K].rearrange("(p t) c -> p t c", t=PACK)[:, 2 * u : 2 * u + 2, :],
+            )
+        ui_rows = sb.tile([P, GATE_TILES - I0, K], BF16)
+        for m in IU_TILES + O_TILES:
+            nc.sync.dma_start(out=ui_rows[:, m - I0, :], in_=U_iou_w[(m - I0) * P : (m - I0 + 1) * P, 0:K])
+
+        ident_f32 = sb.tile([P, P], F32)
+        make_identity(nc, ident_f32[:])
+        ident_bf16 = sb.tile([P, P], BF16)
+        make_identity(nc, ident_bf16[:])
+        warm_in = sb.tile([P, 1], F32)
+        warm_out = sb.tile([P, 1], F32)
+        nc.vector.memset(warm_in[:], 0.0)
+        nc.scalar.activation(out=warm_out[:], in_=warm_in[:], func=ACT.Sigmoid)
+
+        w_grouped = sb.tile([P, GATE_TILES, P * PACK], BF16, align_bytes=64)
+        w_codes = sb.tile([P, GATE_TILES, P], U32, align_bytes=64)
+        w_scales = sb.tile([P, GATE_TILES, P], U8, align_bytes=64)
+        h_grouped = sb.tile([P, P * PACK], BF16, align_bytes=64)
+        h_codes = sb.tile([P, P], U32, align_bytes=64)
+        h_scales = sb.tile([P, P], U8, align_bytes=64)
+        gates = sb.tile([P, GATE_TILES, P], F32)
+
+        def regroup_f(m):
+            nc.vector.tensor_copy(
+                out=w_grouped[:, m, :].rearrange("p (c i t) -> p c t i", i=4, t=PACK),
+                in_=uf_rows[:, :, m * P : (m + 1) * P].rearrange("p t (c i) -> p c t i", i=4),
+            )
+
+        def transpose_iou(m):
+            wT = transpose_words(nc, ps_in, ui_rows[:, m - I0, :], ident_f32)
+            nc.scalar.copy(
+                out=w_grouped[:, m, :].bitcast(F32).rearrange("p (r u) -> p r u", u=2),
+                in_=wT[:].rearrange("p u r -> p r u"),
+            )
+
+        def quantise_weights(m):
+            nc.vector.quantize_mx(
+                out=w_codes[:, m, :].bitcast(FP8X4), scales=w_scales[:, m, :], in_=w_grouped[:, m, :]
+            )
+
+        def gate_group(tiles, bank):
+            for s, m in enumerate(tiles):
+                nc.tensor.matmul_mx(
+                    out=bank[:, s, :],
+                    lhsT=w_codes[:, m, :].bitcast(FP8X4),
+                    lhsT_scale=w_scales[:, m, :],
+                    rhs=h_codes[:].bitcast(FP8X4),
+                    rhs_scale=h_scales[:],
+                    start=True,
+                    stop=True,
+                )
+            for s, m in enumerate(tiles):
+                nc.scalar.activation(
+                    out=gates[:, m, :],
+                    in_=bank[:, s, :],
+                    func=ACT.Tanh if m >= U0 else ACT.Sigmoid,
+                    bias=bias_col[:, m : m + 1],
+                    scale=1.0,
+                )
+
+        hT = transpose_words(nc, ps_in, h_rows[:], ident_f32)
+        nc.scalar.copy(
+            out=h_grouped[:].bitcast(F32).rearrange("p (n u) -> p n u", u=2),
+            in_=hT[:].rearrange("p u n -> p n u"),
+        )
+        nc.vector.quantize_mx(out=h_codes[:].bitcast(FP8X4), scales=h_scales[:], in_=h_grouped[:])
+
+        biasT = ps_in.tile([P, P], BF16, tag="wordsT")
+        nc.tensor.transpose(biasT[:], bias_rows[:], ident_bf16[:])
+        bias_col = sb.tile([P, GATE_TILES], F32)
+        nc.vector.tensor_copy(out=bias_col[:], in_=biasT[:, 0:GATE_TILES])
+
+        cT = ps_keep.tile([P, F_TILES, P], BF16)
+        for m in range(F_TILES):
+            nc.tensor.transpose(cT[:, m, :], c_rows[:, m * P : (m + 1) * P], ident_bf16[:])
+
+        regroup_f(0)
+        for m in range(1, F_TILES):
+            regroup_f(m)
+            quantise_weights(m - 1)
+        quantise_weights(F_TILES - 1)
+
+        for m in IU_TILES:
+            transpose_iou(m)
+            quantise_weights(m)
+        f_bank = ps_bank.tile([P, F_TILES, P], F32, tag="bank")
+        gate_group(range(F_TILES), f_bank)
+        for m in O_TILES:
+            transpose_iou(m)
+        fc = sb.tile([P, F_TILES, P], F32)
+        for a in range(HALVES):
+            nc.vector.tensor_mul(
+                out=fc[:, a:F_TILES:HALVES, :], in0=gates[:, a:F_TILES:HALVES, :], in1=cT[:, a:F_TILES:HALVES, :]
+            )
+        for m in O_TILES:
+            quantise_weights(m)
+        iu_bank = ps_bank.tile([P, len(IU_TILES), P], F32, tag="bank")
+        gate_group(IU_TILES, iu_bank)
+        c_red = sb.tile([P, HALVES, P], F32)
+        for a in range(HALVES):
+            nc.vector.tensor_add(out=c_red[:, a, :], in0=fc[:, a, :], in1=fc[:, HALVES + a, :])
+        o_bank = ps_bank.tile([P, len(O_TILES), P], F32, tag="bank")
+        gate_group(O_TILES, o_bank)
+
+        iu = sb.tile([P, HALVES, P], F32)
+        for a in range(HALVES):
+            nc.vector.tensor_mul(out=iu[:, a, :], in0=gates[:, I0 + a, :], in1=gates[:, U0 + a, :])
+
+        c_back = []
+        for a in range(HALVES):
+            c_back.append(ps_bank.tile([P, P], F32, tag="bank", name="c_back"))
+            nc.tensor.matmul(
+                out=c_back[a][:], lhsT=c_red[:, a, :], rhs=ident_f32[:], is_transpose=True, start=True, stop=False
+            )
+        o_back = ps_bank.tile([P, H], F32, tag="bank")
+        for a in range(HALVES):
+            nc.tensor.matmul(
+                out=c_back[a][:], lhsT=iu[:, a, :], rhs=ident_f32[:], is_transpose=True, start=False, stop=True
+            )
+            nc.tensor.transpose(o_back[:, a * P : (a + 1) * P], gates[:, O0 + a, :], ident_f32[:])
+
+        tanh_c = sb.tile([P, H], F32)
+        for a in range(HALVES):
+            nc.scalar.activation(out=tanh_c[:, a * P : (a + 1) * P], in_=c_back[a][:], func=ACT.Tanh)
+        c_out = sb.tile([P, H], F32)
+        for a in range(HALVES):
+            nc.scalar.copy(out=c_out[:, a * P : (a + 1) * P], in_=c_back[a][:])
+        nc.sync.dma_start(out=out_1, in_=c_out[:])
+
+        h_out = sb.tile([P, H], F32)
+        for a in range(HALVES):
+            half = slice(a * P, (a + 1) * P)
+            nc.vector.tensor_mul(out=h_out[:, half], in0=tanh_c[:, half], in1=o_back[:, half])
+        nc.sync.dma_start(out=out_0, in_=h_out[:])

@@ -18,57 +18,50 @@ HALVES = H // P
 
 F0 = 0
 I0 = 4
-O0 = 6
-U0 = 8
+U0 = 5
+O0 = 8
 F_TILES = 4
 GATE_TILES = 10
-IU_TILES = (I0, U0, I0 + 1, U0 + 1)
-O_TILES = (O0, O0 + 1)
+IU_TILES = (4, 5, 6, 7)
+O_TILES = (8, 9)
+TANH_TILES = (5, 7)
+SOURCE = {4: 0, 5: 4, 6: 1, 7: 5, 8: 2, 9: 3}
 
 FLOPS = 2 * P * K * GATE_TILES * P
 BYTES = 2 * (2 * P * K + K * K + K + 3 * H * K + 3 * H) + 4 * 2 * P * H
-
-
-def transpose_words(nc, psum, rows, ident_f32):
-    words = rows.bitcast(F32)
-    wordsT = psum.tile([P, 2, P], F32, tag="wordsT", name="wordsT")
-    for u in range(2):
-        nc.tensor.transpose(wordsT[:, u, :], words[:, u : 2 * P : 2], ident_f32[:])
-    return wordsT
+SLOT = {m: m if m < I0 else I0 + SOURCE[m] for m in range(GATE_TILES)}
 
 
 def tile_treelstmcell_s_kernel(tc, h_mail, c_mail, U_f_w, U_f_b, U_iou_w, b_iou, out_0, out_1):
     nc = tc.nc
     with ExitStack() as ctx:
         sb = ctx.enter_context(tc.tile_pool(name="sb", bufs=1))
-        ps_in = ctx.enter_context(tc.psum_pool(name="ps_in", bufs=2))
         ps_keep = ctx.enter_context(tc.psum_pool(name="ps_keep", bufs=1))
-        ps_bank = ctx.enter_context(tc.psum_pool(name="ps_bank", bufs=5))
+        ps_bank = ctx.enter_context(tc.psum_pool(name="ps_bank", bufs=7))
         ctx.enter_context(tc.manual_schedule())
 
         bias_rows = sb.tile([P, P], BF16)
         nc.vector.memset(bias_rows[:], 0.0)
-        nc.scalar.dma_start(out=bias_rows[F0:I0, :], in_=U_f_b[0:K].rearrange("(a p) -> a p", p=P))
-        nc.scalar.dma_start(out=bias_rows[I0:GATE_TILES, :], in_=b_iou.rearrange("o (a p) -> (o a) p", p=P))
-
         h_rows = sb.tile([P, K], BF16)
         nc.sync.dma_start(out=h_rows[:], in_=h_mail.rearrange("n k h -> n (k h)"))
+        uf_view = U_f_w[0:K, 0:K].rearrange("(p t) c -> p t c", t=PACK)
+        uf_rows = [sb.tile([P, PACK, K // 2], BF16, name="uf_rows%d" % s) for s in range(2)]
+        ui_view = U_iou_w[:, 0:K].rearrange("(g a p) k -> p g a k", g=3, a=HALVES)
+        ui_rows = [sb.tile([P, 2, K], BF16, name="ui_rows%d" % a) for a in range(3)]
+        nc.sync.dma_start(out=uf_rows[0][:], in_=uf_view[:, :, 0 : K // 2])
+        nc.sync.dma_start(out=bias_rows[F0:I0, :], in_=U_f_b[0:K].rearrange("(a p) -> a p", p=P))
+        nc.sync.dma_start(out=ui_rows[0][:], in_=ui_view[:, 0:3:2, 0, :])
+        nc.sync.dma_start(out=uf_rows[1][:], in_=uf_view[:, :, K // 2 : K])
+        nc.sync.dma_start(out=ui_rows[1][:], in_=ui_view[:, 0:3:2, 1, :])
+        nc.sync.dma_start(out=ui_rows[2][:], in_=ui_view[:, 1, :, :])
         c_rows = sb.tile([P, K], BF16)
         nc.sync.dma_start(out=c_rows[:], in_=c_mail.rearrange("n k h -> n (k h)"))
-        uf_rows = sb.tile([P, PACK, K], BF16)
-        for u in range(2):
-            nc.sync.dma_start(
-                out=uf_rows[:, 2 * u : 2 * u + 2, :],
-                in_=U_f_w[0:K, 0:K].rearrange("(p t) c -> p t c", t=PACK)[:, 2 * u : 2 * u + 2, :],
-            )
-        ui_rows = sb.tile([P, GATE_TILES - I0, K], BF16)
-        for m in IU_TILES + O_TILES:
-            nc.sync.dma_start(out=ui_rows[:, m - I0, :], in_=U_iou_w[(m - I0) * P : (m - I0 + 1) * P, 0:K])
 
         ident_f32 = sb.tile([P, P], F32)
         make_identity(nc, ident_f32[:])
+        nc.gpsimd.dma_start(out=bias_rows[I0:GATE_TILES, :], in_=b_iou.rearrange("o (a p) -> (o a) p", p=P))
         ident_bf16 = sb.tile([P, P], BF16)
-        make_identity(nc, ident_bf16[:])
+        nc.vector.tensor_copy(out=ident_bf16[:], in_=ident_f32[:])
         warm_in = sb.tile([P, 1], F32)
         warm_out = sb.tile([P, 1], F32)
         nc.vector.memset(warm_in[:], 0.0)
@@ -82,25 +75,34 @@ def tile_treelstmcell_s_kernel(tc, h_mail, c_mail, U_f_w, U_f_b, U_iou_w, b_iou,
         h_scales = sb.tile([P, P], U8, align_bytes=64)
         gates = sb.tile([P, GATE_TILES, P], F32)
 
-        def regroup_f(m):
+        def transpose_words(rows):
+            words = rows.bitcast(F32)
+            wordsT = ps_bank.tile([P, 2, P], F32, tag="bank", name="wordsT")
+            for u in range(2):
+                nc.tensor.transpose(wordsT[:, u, :], words[:, u : 2 * P : 2], ident_f32[:])
+            return wordsT
+
+        def interleave_words(copy, out, wordsT):
+            copy(out=out.bitcast(F32).rearrange("p (r u) -> p r u", u=2), in_=wordsT[:].rearrange("p u r -> p r u"))
+
+        def regroup_f(s):
             nc.vector.tensor_copy(
-                out=w_grouped[:, m, :].rearrange("p (c i t) -> p c t i", i=4, t=PACK),
-                in_=uf_rows[:, :, m * P : (m + 1) * P].rearrange("p t (c i) -> p c t i", i=4),
+                out=w_grouped[:, 2 * s : 2 * s + 2, :].rearrange("p m (c i t) -> p (m c) t i", i=4, t=PACK),
+                in_=uf_rows[s][:].rearrange("p t (c i) -> p c t i", i=4),
             )
 
-        def transpose_iou(m):
-            wT = transpose_words(nc, ps_in, ui_rows[:, m - I0, :], ident_f32)
-            nc.scalar.copy(
-                out=w_grouped[:, m, :].bitcast(F32).rearrange("p (r u) -> p r u", u=2),
-                in_=wT[:].rearrange("p u r -> p r u"),
-            )
+        def iou_tile(m, copy):
+            interleave_words(copy, w_grouped[:, m, :], transpose_words(ui_rows[(m - I0) // 2][:, m % 2, :]))
 
-        def quantise_weights(m):
+        def quantise_weights(m0, n):
             nc.vector.quantize_mx(
-                out=w_codes[:, m, :].bitcast(FP8X4), scales=w_scales[:, m, :], in_=w_grouped[:, m, :]
+                out=w_codes[:, m0 : m0 + n, :].rearrange("p m c -> p (m c)").bitcast(FP8X4),
+                scales=w_scales[:, m0 : m0 + n, :].rearrange("p m c -> p (m c)"),
+                in_=w_grouped[:, m0 : m0 + n, :].rearrange("p m c -> p (m c)"),
             )
 
-        def gate_group(tiles, bank):
+        def gate_group(tiles):
+            bank = ps_bank.tile([P, len(tiles), P], F32, tag="bank", name="gate_bank")
             for s, m in enumerate(tiles):
                 nc.tensor.matmul_mx(
                     out=bank[:, s, :],
@@ -111,74 +113,75 @@ def tile_treelstmcell_s_kernel(tc, h_mail, c_mail, U_f_w, U_f_b, U_iou_w, b_iou,
                     start=True,
                     stop=True,
                 )
+            return bank
+
+        def activate(tiles, bank):
             for s, m in enumerate(tiles):
                 nc.scalar.activation(
                     out=gates[:, m, :],
                     in_=bank[:, s, :],
-                    func=ACT.Tanh if m >= U0 else ACT.Sigmoid,
-                    bias=bias_col[:, m : m + 1],
+                    func=ACT.Tanh if m in TANH_TILES else ACT.Sigmoid,
+                    bias=bias_col[:, SLOT[m] : SLOT[m] + 1],
                     scale=1.0,
                 )
 
-        hT = transpose_words(nc, ps_in, h_rows[:], ident_f32)
-        nc.scalar.copy(
-            out=h_grouped[:].bitcast(F32).rearrange("p (n u) -> p n u", u=2),
-            in_=hT[:].rearrange("p u n -> p n u"),
-        )
+        interleave_words(nc.scalar.copy, h_grouped[:], transpose_words(h_rows[:]))
+        regroup_f(0)
         nc.vector.quantize_mx(out=h_codes[:].bitcast(FP8X4), scales=h_scales[:], in_=h_grouped[:])
-
-        biasT = ps_in.tile([P, P], BF16, tag="wordsT")
+        quantise_weights(0, 2)
+        for m in IU_TILES[0:2]:
+            iou_tile(m, nc.scalar.copy)
+        regroup_f(1)
+        quantise_weights(2, 2)
+        quantise_weights(I0, 2)
+        for m in IU_TILES[2:4]:
+            iou_tile(m, nc.scalar.copy)
+        quantise_weights(I0 + 2, 2)
+        for m in O_TILES:
+            iou_tile(m, nc.scalar.copy)
+        biasT = ps_bank.tile([P, P], BF16, tag="bank")
         nc.tensor.transpose(biasT[:], bias_rows[:], ident_bf16[:])
         bias_col = sb.tile([P, GATE_TILES], F32)
         nc.vector.tensor_copy(out=bias_col[:], in_=biasT[:, 0:GATE_TILES])
-
+        f_tiles = (0, 2, 1, 3)
+        f_bank = gate_group(f_tiles)
+        activate(f_tiles, f_bank)
         cT = ps_keep.tile([P, F_TILES, P], BF16)
         for m in range(F_TILES):
             nc.tensor.transpose(cT[:, m, :], c_rows[:, m * P : (m + 1) * P], ident_bf16[:])
+        quantise_weights(O0, 2)
+        iu_banks = [gate_group(IU_TILES[2 * a : 2 * a + 2]) for a in range(HALVES)]
+        for a in range(HALVES):
+            activate(IU_TILES[2 * a : 2 * a + 2], iu_banks[a])
+        o_bank = gate_group(O_TILES)
+        activate(O_TILES, o_bank)
 
-        regroup_f(0)
-        for m in range(1, F_TILES):
-            regroup_f(m)
-            quantise_weights(m - 1)
-        quantise_weights(F_TILES - 1)
-
-        for m in IU_TILES:
-            transpose_iou(m)
-            quantise_weights(m)
-        f_bank = ps_bank.tile([P, F_TILES, P], F32, tag="bank")
-        gate_group(range(F_TILES), f_bank)
-        for m in O_TILES:
-            transpose_iou(m)
         fc = sb.tile([P, F_TILES, P], F32)
+        iu = sb.tile([P, HALVES, P], F32)
         for a in range(HALVES):
             nc.vector.tensor_mul(
                 out=fc[:, a:F_TILES:HALVES, :], in0=gates[:, a:F_TILES:HALVES, :], in1=cT[:, a:F_TILES:HALVES, :]
             )
-        for m in O_TILES:
-            quantise_weights(m)
-        iu_bank = ps_bank.tile([P, len(IU_TILES), P], F32, tag="bank")
-        gate_group(IU_TILES, iu_bank)
-        c_red = sb.tile([P, HALVES, P], F32)
         for a in range(HALVES):
-            nc.vector.tensor_add(out=c_red[:, a, :], in0=fc[:, a, :], in1=fc[:, HALVES + a, :])
-        o_bank = ps_bank.tile([P, len(O_TILES), P], F32, tag="bank")
-        gate_group(O_TILES, o_bank)
+            nc.vector.tensor_mul(out=iu[:, a, :], in0=gates[:, I0 + 2 * a, :], in1=gates[:, U0 + 2 * a, :])
 
-        iu = sb.tile([P, HALVES, P], F32)
+        c_back = [ps_bank.tile([P, P], F32, tag="bank", name="c_back%d" % a) for a in range(HALVES)]
         for a in range(HALVES):
-            nc.vector.tensor_mul(out=iu[:, a, :], in0=gates[:, I0 + a, :], in1=gates[:, U0 + a, :])
-
-        c_back = []
-        for a in range(HALVES):
-            c_back.append(ps_bank.tile([P, P], F32, tag="bank", name="c_back"))
-            nc.tensor.matmul(
-                out=c_back[a][:], lhsT=c_red[:, a, :], rhs=ident_f32[:], is_transpose=True, start=True, stop=False
-            )
-        o_back = ps_bank.tile([P, H], F32, tag="bank")
+            for child in range(2):
+                nc.tensor.matmul(
+                    out=c_back[a][:],
+                    lhsT=fc[:, HALVES * child + a, :],
+                    rhs=ident_f32[:],
+                    is_transpose=True,
+                    start=child == 0,
+                    stop=False,
+                )
         for a in range(HALVES):
             nc.tensor.matmul(
                 out=c_back[a][:], lhsT=iu[:, a, :], rhs=ident_f32[:], is_transpose=True, start=False, stop=True
             )
+        o_back = ps_bank.tile([P, H], F32, tag="bank")
+        for a in range(HALVES):
             nc.tensor.transpose(o_back[:, a * P : (a + 1) * P], gates[:, O0 + a, :], ident_f32[:])
 
         tanh_c = sb.tile([P, H], F32)
@@ -187,7 +190,7 @@ def tile_treelstmcell_s_kernel(tc, h_mail, c_mail, U_f_w, U_f_b, U_iou_w, b_iou,
         c_out = sb.tile([P, H], F32)
         for a in range(HALVES):
             nc.scalar.copy(out=c_out[:, a * P : (a + 1) * P], in_=c_back[a][:])
-        nc.sync.dma_start(out=out_1, in_=c_out[:])
+        nc.scalar.dma_start(out=out_1, in_=c_out[:])
 
         h_out = sb.tile([P, H], F32)
         for a in range(HALVES):

@@ -45,13 +45,15 @@ def tile_treelstmcell_s_kernel(tc, h_mail, c_mail, U_f_w, U_f_b, U_iou_w, b_iou,
         h_rows = sb.tile([P, K], BF16)
         nc.sync.dma_start(out=h_rows[:], in_=h_mail.rearrange("n k h -> n (k h)"))
         uf_view = U_f_w[0:K, 0:K].rearrange("(p t) c -> p t c", t=PACK)
-        uf_rows = [sb.tile([P, PACK, K // 2], BF16, name="uf_rows%d" % s) for s in range(2)]
+        uf_rows = sb.tile([P, PACK, K], BF16)
         ui_view = U_iou_w[:, 0:K].rearrange("(g a p) k -> p g a k", g=3, a=HALVES)
         ui_rows = [sb.tile([P, 2, K], BF16, name="ui_rows%d" % a) for a in range(3)]
-        nc.sync.dma_start(out=uf_rows[0][:], in_=uf_view[:, :, 0 : K // 2])
-        nc.sync.dma_start(out=bias_rows[F0:I0, :], in_=U_f_b[0:K].rearrange("(a p) -> a p", p=P))
+        nc.sync.dma_start(out=uf_rows[:], in_=uf_view)
         nc.sync.dma_start(out=ui_rows[0][:], in_=ui_view[:, 0:3:2, 0, :])
-        nc.sync.dma_start(out=uf_rows[1][:], in_=uf_view[:, :, K // 2 : K])
+        iou_bias = b_iou.rearrange("o (a p) -> (o a) p", p=P)
+        nc.sync.dma_start(out=bias_rows[F0:I0, :], in_=U_f_b[0:K].rearrange("(a p) -> a p", p=P))
+        nc.sync.dma_start(out=bias_rows[I0 : I0 + 4, :], in_=iou_bias[0:4, :])
+        nc.sync.dma_start(out=bias_rows[I0 + 4 : GATE_TILES, :], in_=iou_bias[4:6, :])
         nc.sync.dma_start(out=ui_rows[1][:], in_=ui_view[:, 0:3:2, 1, :])
         nc.sync.dma_start(out=ui_rows[2][:], in_=ui_view[:, 1, :, :])
         c_rows = sb.tile([P, K], BF16)
@@ -59,7 +61,6 @@ def tile_treelstmcell_s_kernel(tc, h_mail, c_mail, U_f_w, U_f_b, U_iou_w, b_iou,
 
         ident_f32 = sb.tile([P, P], F32)
         make_identity(nc, ident_f32[:])
-        nc.gpsimd.dma_start(out=bias_rows[I0:GATE_TILES, :], in_=b_iou.rearrange("o (a p) -> (o a) p", p=P))
         ident_bf16 = sb.tile([P, P], BF16)
         nc.vector.tensor_copy(out=ident_bf16[:], in_=ident_f32[:])
         warm_in = sb.tile([P, 1], F32)
@@ -88,7 +89,7 @@ def tile_treelstmcell_s_kernel(tc, h_mail, c_mail, U_f_w, U_f_b, U_iou_w, b_iou,
         def regroup_f(s):
             nc.vector.tensor_copy(
                 out=w_grouped[:, 2 * s : 2 * s + 2, :].rearrange("p m (c i t) -> p (m c) t i", i=4, t=PACK),
-                in_=uf_rows[s][:].rearrange("p t (c i) -> p c t i", i=4),
+                in_=uf_rows[:, :, 2 * s * P : 2 * (s + 1) * P].rearrange("p t (c i) -> p c t i", i=4),
             )
 
         def iou_tile(m, copy):
@@ -132,17 +133,17 @@ def tile_treelstmcell_s_kernel(tc, h_mail, c_mail, U_f_w, U_f_b, U_iou_w, b_iou,
         for m in IU_TILES[0:2]:
             iou_tile(m, nc.scalar.copy)
         regroup_f(1)
+        biasT = ps_bank.tile([P, P], BF16, tag="bank")
+        nc.tensor.transpose(biasT[:], bias_rows[:], ident_bf16[:])
+        bias_col = sb.tile([P, GATE_TILES], F32)
+        nc.vector.tensor_copy(out=bias_col[:], in_=biasT[:, 0:GATE_TILES])
         quantise_weights(2, 2)
         quantise_weights(I0, 2)
         for m in IU_TILES[2:4]:
             iou_tile(m, nc.scalar.copy)
         quantise_weights(I0 + 2, 2)
         for m in O_TILES:
-            iou_tile(m, nc.scalar.copy)
-        biasT = ps_bank.tile([P, P], BF16, tag="bank")
-        nc.tensor.transpose(biasT[:], bias_rows[:], ident_bf16[:])
-        bias_col = sb.tile([P, GATE_TILES], F32)
-        nc.vector.tensor_copy(out=bias_col[:], in_=biasT[:, 0:GATE_TILES])
+            iou_tile(m, nc.vector.tensor_copy)
         f_tiles = (0, 2, 1, 3)
         f_bank = gate_group(f_tiles)
         activate(f_tiles, f_bank)

@@ -29,7 +29,7 @@ SOURCE = {4: 0, 5: 4, 6: 1, 7: 5, 8: 2, 9: 3}
 
 FLOPS = 2 * P * K * GATE_TILES * P
 BYTES = 2 * (2 * P * K + K * K + K + 3 * H * K + 3 * H) + 4 * 2 * P * H
-SLOT = {m: m if m < I0 else I0 + SOURCE[m] for m in range(GATE_TILES)}
+SLOT = {m: (m % 2, m // 2) if m < I0 else (SOURCE[m] % 3, 2 + SOURCE[m] // 3) for m in range(GATE_TILES)}
 
 
 def tile_treelstmcell_s_kernel(tc, h_mail, c_mail, U_f_w, U_f_b, U_iou_w, b_iou, out_0, out_1):
@@ -40,7 +40,7 @@ def tile_treelstmcell_s_kernel(tc, h_mail, c_mail, U_f_w, U_f_b, U_iou_w, b_iou,
         ps_bank = ctx.enter_context(tc.psum_pool(name="ps_bank", bufs=7))
         ctx.enter_context(tc.manual_schedule())
 
-        bias_rows = sb.tile([P, P], BF16)
+        bias_rows = sb.tile([P, 3 * P], BF16)
         nc.vector.memset(bias_rows[:], 0.0)
         h_rows = sb.tile([P, K], BF16)
         nc.sync.dma_start(out=h_rows[:], in_=h_mail.rearrange("n k h -> n (k h)"))
@@ -49,11 +49,9 @@ def tile_treelstmcell_s_kernel(tc, h_mail, c_mail, U_f_w, U_f_b, U_iou_w, b_iou,
         ui_view = U_iou_w[:, 0:K].rearrange("(g a p) k -> p g a k", g=3, a=HALVES)
         ui_rows = [sb.tile([P, 2, K], BF16, name="ui_rows%d" % a) for a in range(3)]
         nc.sync.dma_start(out=uf_rows[:], in_=uf_view)
+        nc.sync.dma_start(out=bias_rows[0:2, 0 : 2 * P], in_=U_f_b[0:K].rearrange("(r c) -> r c", r=2))
+        nc.sync.dma_start(out=bias_rows[2:4, :], in_=b_iou.rearrange("o (r c) -> (o r) c", r=2))
         nc.sync.dma_start(out=ui_rows[0][:], in_=ui_view[:, 0:3:2, 0, :])
-        iou_bias = b_iou.rearrange("o (a p) -> (o a) p", p=P)
-        nc.sync.dma_start(out=bias_rows[F0:I0, :], in_=U_f_b[0:K].rearrange("(a p) -> a p", p=P))
-        nc.sync.dma_start(out=bias_rows[I0 : I0 + 4, :], in_=iou_bias[0:4, :])
-        nc.sync.dma_start(out=bias_rows[I0 + 4 : GATE_TILES, :], in_=iou_bias[4:6, :])
         nc.sync.dma_start(out=ui_rows[1][:], in_=ui_view[:, 0:3:2, 1, :])
         nc.sync.dma_start(out=ui_rows[2][:], in_=ui_view[:, 1, :, :])
         c_rows = sb.tile([P, K], BF16)
@@ -86,10 +84,10 @@ def tile_treelstmcell_s_kernel(tc, h_mail, c_mail, U_f_w, U_f_b, U_iou_w, b_iou,
         def interleave_words(copy, out, wordsT):
             copy(out=out.bitcast(F32).rearrange("p (r u) -> p r u", u=2), in_=wordsT[:].rearrange("p u r -> p r u"))
 
-        def regroup_f(s):
-            nc.vector.tensor_copy(
-                out=w_grouped[:, 2 * s : 2 * s + 2, :].rearrange("p m (c i t) -> p (m c) t i", i=4, t=PACK),
-                in_=uf_rows[:, :, 2 * s * P : 2 * (s + 1) * P].rearrange("p t (c i) -> p c t i", i=4),
+        def regroup_f(copy, m, n):
+            copy(
+                out=w_grouped[:, m : m + n, :].rearrange("p m (c i t) -> p (m c) t i", i=4, t=PACK),
+                in_=uf_rows[:, :, m * P : (m + n) * P].rearrange("p t (c i) -> p c t i", i=4),
             )
 
         def iou_tile(m, copy):
@@ -122,28 +120,30 @@ def tile_treelstmcell_s_kernel(tc, h_mail, c_mail, U_f_w, U_f_b, U_iou_w, b_iou,
                     out=gates[:, m, :],
                     in_=bank[:, s, :],
                     func=ACT.Tanh if m in TANH_TILES else ACT.Sigmoid,
-                    bias=bias_col[:, SLOT[m] : SLOT[m] + 1],
+                    bias=bias_col[:, SLOT[m][0], SLOT[m][1] : SLOT[m][1] + 1],
                     scale=1.0,
                 )
 
         interleave_words(nc.scalar.copy, h_grouped[:], transpose_words(h_rows[:]))
-        regroup_f(0)
+        regroup_f(nc.vector.tensor_copy, 0, 2)
+        regroup_f(nc.scalar.copy, 3, 1)
         nc.vector.quantize_mx(out=h_codes[:].bitcast(FP8X4), scales=h_scales[:], in_=h_grouped[:])
+        regroup_f(nc.vector.tensor_copy, 2, 1)
         quantise_weights(0, 2)
+        biasT = ps_bank.tile([P, 3, P], BF16, tag="bank")
+        for s in range(3):
+            nc.tensor.transpose(biasT[:, s, :], bias_rows[:, s * P : (s + 1) * P], ident_bf16[:])
+        bias_col = sb.tile([P, 3, 4], F32)
+        nc.vector.tensor_copy(out=bias_col[:], in_=biasT[:, :, 0:4])
         for m in IU_TILES[0:2]:
             iou_tile(m, nc.scalar.copy)
-        regroup_f(1)
-        biasT = ps_bank.tile([P, P], BF16, tag="bank")
-        nc.tensor.transpose(biasT[:], bias_rows[:], ident_bf16[:])
-        bias_col = sb.tile([P, GATE_TILES], F32)
-        nc.vector.tensor_copy(out=bias_col[:], in_=biasT[:, 0:GATE_TILES])
         quantise_weights(2, 2)
         quantise_weights(I0, 2)
         for m in IU_TILES[2:4]:
             iou_tile(m, nc.scalar.copy)
         quantise_weights(I0 + 2, 2)
-        for m in O_TILES:
-            iou_tile(m, nc.vector.tensor_copy)
+        iou_tile(O0, nc.vector.tensor_copy)
+        iou_tile(O0 + 1, nc.scalar.copy)
         f_tiles = (0, 2, 1, 3)
         f_bank = gate_group(f_tiles)
         activate(f_tiles, f_bank)

@@ -42,18 +42,16 @@ def tile_treelstmcell_s_kernel(tc, h_mail, c_mail, U_f_w, U_f_b, U_iou_w, b_iou,
 
         bias_rows = sb.tile([P, 3 * P], BF16)
         nc.vector.memset(bias_rows[:], 0.0)
+        nc.scalar.dma_start(out=bias_rows[0:2, 0 : 2 * P], in_=U_f_b[0:K].rearrange("(r c) -> r c", r=2))
+        nc.scalar.dma_start(out=bias_rows[2:4, :], in_=b_iou.rearrange("o (r c) -> (o r) c", r=2))
         h_rows = sb.tile([P, K], BF16)
         nc.sync.dma_start(out=h_rows[:], in_=h_mail.rearrange("n k h -> n (k h)"))
-        uf_view = U_f_w[0:K, 0:K].rearrange("(p t) c -> p t c", t=PACK)
         uf_rows = sb.tile([P, PACK, K], BF16)
-        ui_view = U_iou_w[:, 0:K].rearrange("(g a p) k -> p g a k", g=3, a=HALVES)
-        ui_rows = [sb.tile([P, 2, K], BF16, name="ui_rows%d" % a) for a in range(3)]
-        nc.sync.dma_start(out=uf_rows[:], in_=uf_view)
-        nc.sync.dma_start(out=bias_rows[0:2, 0 : 2 * P], in_=U_f_b[0:K].rearrange("(r c) -> r c", r=2))
-        nc.sync.dma_start(out=bias_rows[2:4, :], in_=b_iou.rearrange("o (r c) -> (o r) c", r=2))
-        nc.sync.dma_start(out=ui_rows[0][:], in_=ui_view[:, 0:3:2, 0, :])
-        nc.sync.dma_start(out=ui_rows[1][:], in_=ui_view[:, 0:3:2, 1, :])
-        nc.sync.dma_start(out=ui_rows[2][:], in_=ui_view[:, 1, :, :])
+        nc.sync.dma_start(out=uf_rows[:], in_=U_f_w[0:K, 0:K].rearrange("(p t) c -> p t c", t=PACK))
+        ui_rows = {}
+        for m in IU_TILES + O_TILES:
+            ui_rows[m] = sb.tile([P, K], BF16, name="ui_rows%d" % m)
+            nc.sync.dma_start(out=ui_rows[m][:], in_=U_iou_w[SOURCE[m] * P : (SOURCE[m] + 1) * P, 0:K])
         c_rows = sb.tile([P, K], BF16)
         nc.sync.dma_start(out=c_rows[:], in_=c_mail.rearrange("n k h -> n (k h)"))
 
@@ -91,7 +89,7 @@ def tile_treelstmcell_s_kernel(tc, h_mail, c_mail, U_f_w, U_f_b, U_iou_w, b_iou,
             )
 
         def iou_tile(m, copy):
-            interleave_words(copy, w_grouped[:, m, :], transpose_words(ui_rows[(m - I0) // 2][:, m % 2, :]))
+            interleave_words(copy, w_grouped[:, m, :], transpose_words(ui_rows[m][:]))
 
         def quantise_weights(m0, n):
             nc.vector.quantize_mx(
@@ -130,27 +128,28 @@ def tile_treelstmcell_s_kernel(tc, h_mail, c_mail, U_f_w, U_f_b, U_iou_w, b_iou,
         nc.vector.quantize_mx(out=h_codes[:].bitcast(FP8X4), scales=h_scales[:], in_=h_grouped[:])
         regroup_f(nc.vector.tensor_copy, 2, 1)
         quantise_weights(0, 2)
+        for m in IU_TILES[0:2]:
+            iou_tile(m, nc.scalar.copy)
         biasT = ps_bank.tile([P, 3, P], BF16, tag="bank")
         for s in range(3):
             nc.tensor.transpose(biasT[:, s, :], bias_rows[:, s * P : (s + 1) * P], ident_bf16[:])
         bias_col = sb.tile([P, 3, 4], F32)
         nc.vector.tensor_copy(out=bias_col[:], in_=biasT[:, :, 0:4])
-        for m in IU_TILES[0:2]:
-            iou_tile(m, nc.scalar.copy)
         quantise_weights(2, 2)
         quantise_weights(I0, 2)
         for m in IU_TILES[2:4]:
             iou_tile(m, nc.scalar.copy)
         quantise_weights(I0 + 2, 2)
-        iou_tile(O0, nc.vector.tensor_copy)
-        iou_tile(O0 + 1, nc.scalar.copy)
+        iou_tile(O0, nc.scalar.copy)
+        quantise_weights(O0, 1)
+        iou_tile(O0 + 1, nc.vector.tensor_copy)
         f_tiles = (0, 2, 1, 3)
         f_bank = gate_group(f_tiles)
         activate(f_tiles, f_bank)
         cT = ps_keep.tile([P, F_TILES, P], BF16)
         for m in range(F_TILES):
             nc.tensor.transpose(cT[:, m, :], c_rows[:, m * P : (m + 1) * P], ident_bf16[:])
-        quantise_weights(O0, 2)
+        quantise_weights(O0 + 1, 1)
         iu_banks = [gate_group(IU_TILES[2 * a : 2 * a + 2]) for a in range(HALVES)]
         for a in range(HALVES):
             activate(IU_TILES[2 * a : 2 * a + 2], iu_banks[a])

@@ -42,16 +42,27 @@ def tile_treelstmcell_s_kernel(tc, h_mail, c_mail, U_f_w, U_f_b, U_iou_w, b_iou,
 
         bias_rows = sb.tile([P, 3 * P], BF16)
         nc.vector.memset(bias_rows[:], 0.0)
-        nc.scalar.dma_start(out=bias_rows[0:2, 0 : 2 * P], in_=U_f_b[0:K].rearrange("(r c) -> r c", r=2))
-        nc.scalar.dma_start(out=bias_rows[2:4, :], in_=b_iou.rearrange("o (r c) -> (o r) c", r=2))
         h_rows = sb.tile([P, K], BF16)
         nc.sync.dma_start(out=h_rows[:], in_=h_mail.rearrange("n k h -> n (k h)"))
         uf_rows = sb.tile([P, PACK, K], BF16)
         nc.sync.dma_start(out=uf_rows[:], in_=U_f_w[0:K, 0:K].rearrange("(p t) c -> p t c", t=PACK))
         ui_rows = {}
-        for m in IU_TILES + O_TILES:
-            ui_rows[m] = sb.tile([P, K], BF16, name="ui_rows%d" % m)
-            nc.sync.dma_start(out=ui_rows[m][:], in_=U_iou_w[SOURCE[m] * P : (SOURCE[m] + 1) * P, 0:K])
+
+        def load_iou(m):
+            rows = sb.tile([P, K], BF16, name="ui_rows%d" % m)
+            ui_rows[m] = rows[:]
+            nc.sync.dma_start(out=rows[:], in_=U_iou_w[SOURCE[m] * P : (SOURCE[m] + 1) * P, 0:K])
+
+        for m in IU_TILES[0:2]:
+            load_iou(m)
+        nc.sync.dma_start(out=bias_rows[0:2, 0 : 2 * P], in_=U_f_b[0:K].rearrange("(r c) -> r c", r=2))
+        nc.sync.dma_start(out=bias_rows[2:4, :], in_=b_iou.rearrange("o (r c) -> (o r) c", r=2))
+        pair = sb.tile([P, 2, K], BF16)
+        nc.sync.dma_start(out=pair[:], in_=U_iou_w[:, 0:K].rearrange("(g a p) k -> p g a k", g=3, a=HALVES)[:, 0:3:2, 1, :])
+        for s, m in enumerate(IU_TILES[2:4]):
+            ui_rows[m] = pair[:, s, :]
+        for m in O_TILES:
+            load_iou(m)
         c_rows = sb.tile([P, K], BF16)
         nc.sync.dma_start(out=c_rows[:], in_=c_mail.rearrange("n k h -> n (k h)"))
 
@@ -59,10 +70,8 @@ def tile_treelstmcell_s_kernel(tc, h_mail, c_mail, U_f_w, U_f_b, U_iou_w, b_iou,
         make_identity(nc, ident_f32[:])
         ident_bf16 = sb.tile([P, P], BF16)
         nc.vector.tensor_copy(out=ident_bf16[:], in_=ident_f32[:])
-        warm_in = sb.tile([P, 1], F32)
-        warm_out = sb.tile([P, 1], F32)
-        nc.vector.memset(warm_in[:], 0.0)
-        nc.scalar.activation(out=warm_out[:], in_=warm_in[:], func=ACT.Sigmoid)
+        warm_rows = sb.tile([P, P], F32)
+        nc.scalar.activation(out=warm_rows[:], in_=ident_f32[:], func=ACT.Sigmoid)
 
         w_grouped = sb.tile([P, GATE_TILES, P * PACK], BF16, align_bytes=64)
         w_codes = sb.tile([P, GATE_TILES, P], U32, align_bytes=64)
@@ -89,7 +98,7 @@ def tile_treelstmcell_s_kernel(tc, h_mail, c_mail, U_f_w, U_f_b, U_iou_w, b_iou,
             )
 
         def iou_tile(m, copy):
-            interleave_words(copy, w_grouped[:, m, :], transpose_words(ui_rows[m][:]))
+            interleave_words(copy, w_grouped[:, m, :], transpose_words(ui_rows[m]))
 
         def quantise_weights(m0, n):
             nc.vector.quantize_mx(
@@ -122,7 +131,14 @@ def tile_treelstmcell_s_kernel(tc, h_mail, c_mail, U_f_w, U_f_b, U_iou_w, b_iou,
                     scale=1.0,
                 )
 
+        def warm_tensor_engine(n):
+            for i in range(n):
+                scratch = ps_bank.tile([P, P], F32, tag="bank", name="scratch")
+                nc.tensor.matmul(out=scratch[:], lhsT=ident_f32[:], rhs=warm_rows[:], start=True, stop=True)
+
+        warm_tensor_engine(2)
         interleave_words(nc.scalar.copy, h_grouped[:], transpose_words(h_rows[:]))
+        warm_tensor_engine(2)
         regroup_f(nc.vector.tensor_copy, 0, 2)
         regroup_f(nc.scalar.copy, 3, 1)
         nc.vector.quantize_mx(out=h_codes[:].bitcast(FP8X4), scales=h_scales[:], in_=h_grouped[:])
@@ -162,38 +178,30 @@ def tile_treelstmcell_s_kernel(tc, h_mail, c_mail, U_f_w, U_f_b, U_iou_w, b_iou,
             nc.vector.tensor_mul(
                 out=fc[:, a:F_TILES:HALVES, :], in0=gates[:, a:F_TILES:HALVES, :], in1=cT[:, a:F_TILES:HALVES, :]
             )
-        for a in range(HALVES):
             nc.vector.tensor_mul(out=iu[:, a, :], in0=gates[:, I0 + 2 * a, :], in1=gates[:, U0 + 2 * a, :])
 
         c_back = [ps_bank.tile([P, P], F32, tag="bank", name="c_back%d" % a) for a in range(HALVES)]
+        o_back = [ps_bank.tile([P, P], F32, tag="bank", name="o_back%d" % a) for a in range(HALVES)]
         for a in range(HALVES):
-            for child in range(2):
+            terms = [fc[:, a, :], fc[:, HALVES + a, :], iu[:, a, :]]
+            for n, term in enumerate(terms):
                 nc.tensor.matmul(
                     out=c_back[a][:],
-                    lhsT=fc[:, HALVES * child + a, :],
+                    lhsT=term,
                     rhs=ident_f32[:],
                     is_transpose=True,
-                    start=child == 0,
-                    stop=False,
+                    start=n == 0,
+                    stop=n == len(terms) - 1,
                 )
-        for a in range(HALVES):
-            nc.tensor.matmul(
-                out=c_back[a][:], lhsT=iu[:, a, :], rhs=ident_f32[:], is_transpose=True, start=False, stop=True
-            )
-        o_back = ps_bank.tile([P, H], F32, tag="bank")
-        for a in range(HALVES):
-            nc.tensor.transpose(o_back[:, a * P : (a + 1) * P], gates[:, O0 + a, :], ident_f32[:])
+            nc.tensor.transpose(o_back[a][:], gates[:, O0 + a, :], ident_f32[:])
 
-        tanh_c = sb.tile([P, H], F32)
-        for a in range(HALVES):
-            nc.scalar.activation(out=tanh_c[:, a * P : (a + 1) * P], in_=c_back[a][:], func=ACT.Tanh)
-        c_out = sb.tile([P, H], F32)
-        for a in range(HALVES):
-            nc.scalar.copy(out=c_out[:, a * P : (a + 1) * P], in_=c_back[a][:])
-        nc.scalar.dma_start(out=out_1, in_=c_out[:])
-
-        h_out = sb.tile([P, H], F32)
         for a in range(HALVES):
             half = slice(a * P, (a + 1) * P)
-            nc.vector.tensor_mul(out=h_out[:, half], in0=tanh_c[:, half], in1=o_back[:, half])
-        nc.sync.dma_start(out=out_0, in_=h_out[:])
+            tanh_c = sb.tile([P, P], F32, name="tanh_c%d" % a)
+            c_out = sb.tile([P, P], F32, name="c_out%d" % a)
+            h_out = sb.tile([P, P], F32, name="h_out%d" % a)
+            nc.scalar.activation(out=tanh_c[:], in_=c_back[a][:], func=ACT.Tanh)
+            nc.scalar.copy(out=c_out[:], in_=c_back[a][:])
+            nc.sync.dma_start(out=out_1[:, half], in_=c_out[:])
+            nc.vector.tensor_mul(out=h_out[:], in0=tanh_c[:], in1=o_back[a][:])
+            nc.sync.dma_start(out=out_0[:, half], in_=h_out[:])

from contextlib import ExitStack

import concourse.mybir as mybir
from concourse.masks import make_identity

F32 = mybir.dt.float32
BF16 = mybir.dt.bfloat16
U32 = mybir.dt.uint32
U8 = mybir.dt.uint8
FP8X4 = mybir.dt.float8_e4m3fn_x4
ACT = mybir.ActivationFunctionType

P = 128
PACK = 4
K = P * PACK
H = 256
HALVES = H // P

F0 = 0
I0 = 4
U0 = 5
O0 = 8
F_TILES = 4
GATE_TILES = 10
IU_TILES = (4, 5, 6, 7)
O_TILES = (8, 9)
TANH_TILES = (5, 7)
SOURCE = {4: 0, 5: 4, 6: 1, 7: 5, 8: 2, 9: 3}

FLOPS = 2 * P * K * GATE_TILES * P
BYTES = 2 * (2 * P * K + K * K + K + 3 * H * K + 3 * H) + 4 * 2 * P * H
SLOT = {m: (m % 2, m // 2) if m < I0 else (SOURCE[m] % 3, 2 + SOURCE[m] // 3) for m in range(GATE_TILES)}


def tile_treelstmcell_s_kernel(tc, h_mail, c_mail, U_f_w, U_f_b, U_iou_w, b_iou, out_0, out_1):
    nc = tc.nc
    with ExitStack() as ctx:
        sb = ctx.enter_context(tc.tile_pool(name="sb", bufs=1))
        ps_keep = ctx.enter_context(tc.psum_pool(name="ps_keep", bufs=1))
        ps_bank = ctx.enter_context(tc.psum_pool(name="ps_bank", bufs=7))
        ctx.enter_context(tc.manual_schedule())

        bias_rows = sb.tile([P, 3 * P], BF16)
        nc.vector.memset(bias_rows[:], 0.0)
        h_rows = sb.tile([P, K], BF16)
        nc.sync.dma_start(out=h_rows[:], in_=h_mail.rearrange("n k h -> n (k h)"))
        uf_rows = sb.tile([P, PACK, K], BF16)
        nc.sync.dma_start(out=uf_rows[:], in_=U_f_w[0:K, 0:K].rearrange("(p t) c -> p t c", t=PACK))
        ui_rows = {}

        def load_iou(m):
            rows = sb.tile([P, K], BF16, name="ui_rows%d" % m)
            ui_rows[m] = rows[:]
            nc.sync.dma_start(out=rows[:], in_=U_iou_w[SOURCE[m] * P : (SOURCE[m] + 1) * P, 0:K])

        for m in IU_TILES[0:2]:
            load_iou(m)
        nc.sync.dma_start(out=bias_rows[0:2, 0 : 2 * P], in_=U_f_b[0:K].rearrange("(r c) -> r c", r=2))
        nc.sync.dma_start(out=bias_rows[2:4, :], in_=b_iou.rearrange("o (r c) -> (o r) c", r=2))
        pair = sb.tile([P, 2, K], BF16)
        nc.sync.dma_start(out=pair[:], in_=U_iou_w[:, 0:K].rearrange("(g a p) k -> p g a k", g=3, a=HALVES)[:, 0:3:2, 1, :])
        for s, m in enumerate(IU_TILES[2:4]):
            ui_rows[m] = pair[:, s, :]
        for m in O_TILES:
            load_iou(m)
        c_rows = sb.tile([P, K], BF16)
        nc.sync.dma_start(out=c_rows[:], in_=c_mail.rearrange("n k h -> n (k h)"))

        ident_f32 = sb.tile([P, P], F32)
        make_identity(nc, ident_f32[:])
        ident_bf16 = sb.tile([P, P], BF16)
        nc.vector.tensor_copy(out=ident_bf16[:], in_=ident_f32[:])
        warm_rows = sb.tile([P, P], F32)
        nc.scalar.activation(out=warm_rows[:], in_=ident_f32[:], func=ACT.Sigmoid)

        w_grouped = sb.tile([P, GATE_TILES, P * PACK], BF16, align_bytes=64)
        w_codes = sb.tile([P, GATE_TILES, P], U32, align_bytes=64)
        w_scales = sb.tile([P, GATE_TILES, P], U8, align_bytes=64)
        h_grouped = sb.tile([P, P * PACK], BF16, align_bytes=64)
        h_codes = sb.tile([P, P], U32, align_bytes=64)
        h_scales = sb.tile([P, P], U8, align_bytes=64)
        gates = sb.tile([P, GATE_TILES, P], F32)

        def transpose_words(rows):
            words = rows.bitcast(F32)
            wordsT = ps_bank.tile([P, 2, P], F32, tag="bank", name="wordsT")
            for u in range(2):
                nc.tensor.transpose(wordsT[:, u, :], words[:, u : 2 * P : 2], ident_f32[:])
            return wordsT

        def interleave_words(copy, out, wordsT):
            copy(out=out.bitcast(F32).rearrange("p (r u) -> p r u", u=2), in_=wordsT[:].rearrange("p u r -> p r u"))

        def regroup_f(copy, m, n):
            copy(
                out=w_grouped[:, m : m + n, :].rearrange("p m (c i t) -> p (m c) t i", i=4, t=PACK),
                in_=uf_rows[:, :, m * P : (m + n) * P].rearrange("p t (c i) -> p c t i", i=4),
            )

        def iou_tile(m, copy):
            interleave_words(copy, w_grouped[:, m, :], transpose_words(ui_rows[m]))

        def quantise_weights(m0, n):
            nc.vector.quantize_mx(
                out=w_codes[:, m0 : m0 + n, :].rearrange("p m c -> p (m c)").bitcast(FP8X4),
                scales=w_scales[:, m0 : m0 + n, :].rearrange("p m c -> p (m c)"),
                in_=w_grouped[:, m0 : m0 + n, :].rearrange("p m c -> p (m c)"),
            )

        def gate_group(tiles):
            bank = ps_bank.tile([P, len(tiles), P], F32, tag="bank", name="gate_bank")
            for s, m in enumerate(tiles):
                nc.tensor.matmul_mx(
                    out=bank[:, s, :],
                    lhsT=w_codes[:, m, :].bitcast(FP8X4),
                    lhsT_scale=w_scales[:, m, :],
                    rhs=h_codes[:].bitcast(FP8X4),
                    rhs_scale=h_scales[:],
                    start=True,
                    stop=True,
                )
            return bank

        def activate(tiles, bank):
            for s, m in enumerate(tiles):
                nc.scalar.activation(
                    out=gates[:, m, :],
                    in_=bank[:, s, :],
                    func=ACT.Tanh if m in TANH_TILES else ACT.Sigmoid,
                    bias=bias_col[:, SLOT[m][0], SLOT[m][1] : SLOT[m][1] + 1],
                    scale=1.0,
                )

        def warm_tensor_engine(n):
            for i in range(n):
                scratch = ps_bank.tile([P, P], F32, tag="bank", name="scratch")
                nc.tensor.matmul(out=scratch[:], lhsT=ident_f32[:], rhs=warm_rows[:], start=True, stop=True)

        warm_tensor_engine(2)
        interleave_words(nc.scalar.copy, h_grouped[:], transpose_words(h_rows[:]))
        warm_tensor_engine(2)
        regroup_f(nc.vector.tensor_copy, 0, 2)
        regroup_f(nc.scalar.copy, 3, 1)
        nc.vector.quantize_mx(out=h_codes[:].bitcast(FP8X4), scales=h_scales[:], in_=h_grouped[:])
        regroup_f(nc.vector.tensor_copy, 2, 1)
        quantise_weights(0, 2)
        for m in IU_TILES[0:2]:
            iou_tile(m, nc.scalar.copy)
        biasT = ps_bank.tile([P, 3, P], BF16, tag="bank")
        for s in range(3):
            nc.tensor.transpose(biasT[:, s, :], bias_rows[:, s * P : (s + 1) * P], ident_bf16[:])
        bias_col = sb.tile([P, 3, 4], F32)
        nc.vector.tensor_copy(out=bias_col[:], in_=biasT[:, :, 0:4])
        quantise_weights(2, 2)
        quantise_weights(I0, 2)
        for m in IU_TILES[2:4]:
            iou_tile(m, nc.scalar.copy)
        quantise_weights(I0 + 2, 2)
        iou_tile(O0, nc.scalar.copy)
        quantise_weights(O0, 1)
        iou_tile(O0 + 1, nc.vector.tensor_copy)
        f_tiles = (0, 2, 1, 3)
        f_bank = gate_group(f_tiles)
        activate(f_tiles, f_bank)
        cT = ps_keep.tile([P, F_TILES, P], BF16)
        for m in range(F_TILES):
            nc.tensor.transpose(cT[:, m, :], c_rows[:, m * P : (m + 1) * P], ident_bf16[:])
        quantise_weights(O0 + 1, 1)
        iu_banks = [gate_group(IU_TILES[2 * a : 2 * a + 2]) for a in range(HALVES)]
        for a in range(HALVES):
            activate(IU_TILES[2 * a : 2 * a + 2], iu_banks[a])
        o_bank = gate_group(O_TILES)
        activate(O_TILES, o_bank)

        fc = sb.tile([P, F_TILES, P], F32)
        iu = sb.tile([P, HALVES, P], F32)
        for a in range(HALVES):
            nc.vector.tensor_mul(
                out=fc[:, a:F_TILES:HALVES, :], in0=gates[:, a:F_TILES:HALVES, :], in1=cT[:, a:F_TILES:HALVES, :]
            )
            nc.vector.tensor_mul(out=iu[:, a, :], in0=gates[:, I0 + 2 * a, :], in1=gates[:, U0 + 2 * a, :])

        c_back = [ps_bank.tile([P, P], F32, tag="bank", name="c_back%d" % a) for a in range(HALVES)]
        o_back = [ps_bank.tile([P, P], F32, tag="bank", name="o_back%d" % a) for a in range(HALVES)]
        for a in range(HALVES):
            terms = [fc[:, a, :], fc[:, HALVES + a, :], iu[:, a, :]]
            for n, term in enumerate(terms):
                nc.tensor.matmul(
                    out=c_back[a][:],
                    lhsT=term,
                    rhs=ident_f32[:],
                    is_transpose=True,
                    start=n == 0,
                    stop=n == len(terms) - 1,
                )
            nc.tensor.transpose(o_back[a][:], gates[:, O0 + a, :], ident_f32[:])

        for a in range(HALVES):
            half = slice(a * P, (a + 1) * P)
            tanh_c = sb.tile([P, P], F32, name="tanh_c%d" % a)
            c_out = sb.tile([P, P], F32, name="c_out%d" % a)
            h_out = sb.tile([P, P], F32, name="h_out%d" % a)
            nc.scalar.activation(out=tanh_c[:], in_=c_back[a][:], func=ACT.Tanh)
            nc.scalar.copy(out=c_out[:], in_=c_back[a][:])
            nc.sync.dma_start(out=out_1[:, half], in_=c_out[:])
            nc.vector.tensor_mul(out=h_out[:], in0=tanh_c[:], in1=o_back[a][:])
            nc.sync.dma_start(out=out_0[:, half], in_=h_out[:])
